import numpy as np
import ml_dtypes


def mxq(x, axis, fmt="e4m3"):
    dtype, down = {"e4m3": (ml_dtypes.float8_e4m3fn, 7), "e5m2": (ml_dtypes.float8_e5m2, 14)}[fmt]
    v = np.moveaxis(np.asarray(x, np.float32).astype(ml_dtypes.bfloat16).astype(np.float64), axis, -1)
    blocks = v.reshape(v.shape[:-1] + (-1, 32))
    amax = np.abs(blocks).max(-1, keepdims=True)
    byte = np.maximum(np.where(amax > 0, np.frexp(amax)[1] - 1 + 127, 0) - down, 1)
    scale = np.exp2(byte - 127.0)
    codes = (blocks / scale).astype(np.float32).astype(dtype).astype(np.float64)
    return np.moveaxis((codes * scale).reshape(v.shape), -1, axis)


WIDE = False


def mx_kscale(k):
    if not WIDE:
        return np.ones(k)
    levels = np.array([10, -10, 5, -5, 0])
    if k % 512:
        return np.exp2(np.random.permutation(np.resize(levels, k // 32))).repeat(32)
    a = np.empty((k // 512, 16))
    for p in range(k // 512):
        a[p, :8] = np.random.permutation(np.resize(levels, 8))
        for g in range(8):
            far = levels[np.abs(levels - a[p, g]) >= 10]
            a[p, g + 8] = far[np.random.randint(len(far))]
    return np.exp2(a.ravel()).repeat(32)


BF16 = ml_dtypes.bfloat16


def bf(x):
    return np.asarray(x, np.float32).astype(BF16)


def f64(x):
    return np.asarray(x).astype(np.float64)


B, N, D, H, S = 4, 1024, 1024, 384, 256
E = 2 * H + S
EPS = 1e-5


def silu(z):
    return z / (1.0 + np.exp(-z))


def setup_inputs():
    s = mx_kscale(D)
    c = np.exp2(np.round(np.log2(np.sqrt(np.mean(s * s)))))
    rows = np.exp(0.5 * np.random.standard_normal((B, N, 1)))
    return {"x": bf(np.random.standard_normal((B, N, D)) * rows * s),
            "g": bf(1.3 + 0.05 * np.random.standard_normal(1)),
            "W_uv": bf(np.random.standard_normal((D, E)) * 0.55 / np.sqrt(D) / s[:, None] * c),
            "b_uv": bf(0.1 * np.random.standard_normal(E)),
            "gamma": bf(1.0 + 0.1 * np.random.standard_normal((2, S))),
            "beta": bf(0.1 * np.random.standard_normal((2, S)))}


def reference(x, g, W_uv, b_uv, gamma, beta):
    x, g, gamma, beta = f64(x), f64(g), f64(gamma), f64(beta)
    norm = np.sqrt((x * x).sum(-1, keepdims=True)) * (1.0 / np.sqrt(D))
    xn = x / np.maximum(norm, EPS) * g
    uv = silu((mxq(xn, 2, "e4m3") @ mxq(f64(W_uv), 0, "e4m3")) + f64(b_uv))
    u = uv[..., :H]
    v = uv[..., H:2 * H]
    base = uv[..., 2 * H:]
    q = base * gamma[0] + beta[0]
    k = base * gamma[1] + beta[1]
    return u, v, q, k

@@ -1,0 +1,390 @@
+from contextlib import ExitStack
+
+import concourse.mybir as mybir
+from concourse.masks import make_identity
+
+F32 = mybir.dt.float32
+BF16 = mybir.dt.bfloat16
+U32 = mybir.dt.uint32
+U8 = mybir.dt.uint8
+FP8X4 = mybir.dt.float8_e4m3fn_x4
+ACT = mybir.ActivationFunctionType
+ALU = mybir.AluOpType
+
+P = 128
+TOKENS = 4 * 1024
+D = 1024
+H = 384
+S = 256
+E = 2 * H + S
+EPS = 1e-5
+
+PACK = 4
+K_PASS = PACK * P
+PASSES = D // K_PASS
+N_BANK = 512
+N_TAIL = 2 * H - N_BANK
+WORD_BLOCKS = D // 2 // P
+BASE_BLOCKS = S // P
+
+TILES = TOKENS // P
+RUN = 2
+RUN_TOKENS = RUN * P
+RUNS = TILES // RUN
+
+BIAS_ROW = 0
+GAMMA_ROW = BIAS_ROW + BASE_BLOCKS
+BETA_ROW = GAMMA_ROW + 2 * BASE_BLOCKS
+CONST_ROWS = BETA_ROW + 2 * BASE_BLOCKS
+
+FLOPS = 2 * TOKENS * D * E
+
+
+def tile_gatedattentionunit_pa_t_kernel(
+    tc, x, g, W_uv, b_uv, gamma, beta, out_0, out_1, out_2, out_3
+):
+    nc = tc.nc
+    x_rows = x.flatten_outer_dims()
+    u_rows = out_0.flatten_outer_dims()
+    v_rows = out_1.flatten_outer_dims()
+    q_rows = out_2.flatten_outer_dims()
+    k_rows = out_3.flatten_outer_dims()
+
+    with ExitStack() as stack:
+        const = stack.enter_context(tc.tile_pool(name="const", bufs=1))
+        x_pool = stack.enter_context(tc.tile_pool(name="x_pool", bufs=1))
+        w_stage = stack.enter_context(tc.tile_pool(name="w_stage", bufs=4))
+        front = stack.enter_context(tc.tile_pool(name="front", bufs=4))
+        back = stack.enter_context(tc.tile_pool(name="back", bufs=3))
+        outs = stack.enter_context(tc.tile_pool(name="outs", bufs=4))
+        psum_t = stack.enter_context(tc.psum_pool(name="psum_t", bufs=4))
+        psum_head = stack.enter_context(tc.psum_pool(name="psum_head", bufs=2))
+        psum_tail = stack.enter_context(tc.psum_pool(name="psum_tail", bufs=1))
+        psum_base = stack.enter_context(tc.psum_pool(name="psum_base", bufs=1))
+        stack.enter_context(tc.manual_schedule())
+
+        def run_rows(dram, r):
+            return dram[r * RUN_TOKENS : (r + 1) * RUN_TOKENS, :].rearrange(
+                "(p s) n -> p s n", s=RUN
+            )
+
+        def load_x(r):
+            x_run = x_pool.tile([P, RUN, D], BF16, name="x_run%d" % r)
+            nc.sync.dma_start(out=x_run[:], in_=run_rows(x_rows, r))
+            return x_run
+
+        w_raw = const.tile([P, PASSES, PACK, E], BF16)
+
+        def load_w(c):
+            nc.sync.dma_start(
+                out=w_raw[:, c, :, :],
+                in_=W_uv[c * K_PASS : (c + 1) * K_PASS, :].rearrange("(p j) n -> p j n", j=PACK),
+            )
+
+        x_sb = [load_x(0)]
+        load_w(0)
+        x_sb.append(load_x(1))
+        load_w(1)
+        for r in range(2, RUNS):
+            x_sb.append(load_x(r))
+
+        g_bf = const.tile([P, 1], BF16)
+        nc.scalar.dma_start(out=g_bf[:], in_=g.partition_broadcast(P))
+        uv_bias_row = const.tile([P, 2 * H], BF16)
+        nc.vector.memset(uv_bias_row[:], 0.0)
+        nc.scalar.dma_start(out=uv_bias_row[0:1, :], in_=b_uv[0 : 2 * H].unsqueeze(0))
+        base_rows = const.tile([P, P], BF16)
+        nc.vector.memset(base_rows[:], 0.0)
+        nc.scalar.dma_start(
+            out=base_rows[BIAS_ROW:GAMMA_ROW, :],
+            in_=b_uv[2 * H : E].rearrange("(b n) -> b n", n=P),
+        )
+        nc.scalar.dma_start(
+            out=base_rows[GAMMA_ROW:BETA_ROW, :],
+            in_=gamma.rearrange("a (b n) -> (a b) n", n=P),
+        )
+        nc.scalar.dma_start(
+            out=base_rows[BETA_ROW:CONST_ROWS, :],
+            in_=beta.rearrange("a (b n) -> (a b) n", n=P),
+        )
+
+        warm = const.tile([P, 1], F32)
+        nc.vector.memset(warm[:], 0.0)
+        nc.scalar.activation(out=warm[:], in_=warm[:], func=ACT.Silu)
+
+        ident = const.tile([P, P], F32)
+        make_identity(nc, ident[:])
+        ident_bf = const.tile([P, P], BF16)
+        make_identity(nc, ident_bf[:])
+        neg_half = const.tile([P, RUN], F32)
+        nc.gpsimd.memset(neg_half[:], -0.5)
+        g_f32 = const.tile([P, 1], F32)
+        nc.vector.tensor_copy(out=g_f32[:], in_=g_bf[:])
+
+        ones = const.tile([P, P], BF16)
+        nc.vector.memset(ones[:], 1.0)
+        uv_bias = const.tile([P, 2 * H], F32)
+        for first, width in ((0, N_BANK), (N_BANK, N_TAIL)):
+            spread = psum_head.tile([P, N_BANK], F32, name="head")
+            nc.tensor.matmul(
+                out=spread[:, 0:width],
+                lhsT=ones[:],
+                rhs=uv_bias_row[:, first : first + width],
+                start=True,
+                stop=True,
+            )
+            nc.vector.tensor_copy(
+                out=uv_bias[:, first : first + width], in_=spread[:, 0:width]
+            )
+        base_cols_ps = psum_t.tile([P, P], BF16, name="bank_t")
+        nc.tensor.transpose(base_cols_ps[:], base_rows[:], ident_bf[:])
+        base_cols = const.tile([P, CONST_ROWS], F32)
+        nc.vector.tensor_copy(out=base_cols[:], in_=base_cols_ps[:, 0:CONST_ROWS])
+
+        def base_const(first_row, a, b):
+            row = first_row + a * BASE_BLOCKS + b
+            return base_cols[:, row : row + 1]
+
+        w_codes = const.tile([P, PASSES, E], U32, align_bytes=64)
+        w_scales = const.tile([P, PASSES, E], U8, align_bytes=64)
+        w_grouped = {}
+
+        def group_w(c):
+            for half, copy in enumerate((nc.vector.tensor_copy, nc.scalar.copy)):
+                w_grouped[c, half] = w_stage.tile(
+                    [P, N_BANK, PACK], BF16, name="w_grouped", align_bytes=64
+                )
+                copy(
+                    out=w_grouped[c, half][:].rearrange("p (n m) j -> p n j m", m=4),
+                    in_=w_raw[:, c, :, half * N_BANK : (half + 1) * N_BANK].rearrange(
+                        "p j (n m) -> p n j m", m=4
+                    ),
+                )
+
+        def quantise_w(c):
+            for half in range(E // N_BANK):
+                cols = slice(half * N_BANK, (half + 1) * N_BANK)
+                nc.vector.quantize_mx(
+                    out=w_codes[:, c, cols].bitcast(FP8X4),
+                    scales=w_scales[:, c, cols],
+                    in_=w_grouped[c, half][:].rearrange("p n j -> p (n j)"),
+                )
+
+        sumsq = const.tile([P, TILES], F32)
+        meansq = const.tile([P, TILES], F32)
+        rnorm = const.tile([P, TILES], F32)
+        xn = {}
+        x_banks = {}
+        x_codes = {}
+        x_scales = {}
+        qk_t = {}
+        qk_banks = {}
+        grouped = {}
+        z = {}
+
+        def x_tile(i):
+            return x_sb[i // RUN][:, i % RUN, :]
+
+        def norm(r):
+            for i in range(r * RUN, (r + 1) * RUN):
+                squares = front.tile([P, D], BF16, bufs=2)
+                nc.scalar.activation(
+                    out=squares[:],
+                    in_=x_tile(i),
+                    func=ACT.Square,
+                    accum_out=sumsq[:, i : i + 1],
+                )
+            cols = slice(r * RUN, (r + 1) * RUN)
+            nc.gpsimd.tensor_scalar(
+                out=meansq[:, cols],
+                in0=sumsq[:, cols],
+                scalar1=1.0 / D,
+                scalar2=EPS * EPS,
+                op0=ALU.mult,
+                op1=ALU.max,
+            )
+            nc.gpsimd.tensor_tensor(
+                out=rnorm[:, cols], in0=meansq[:, cols], in1=neg_half[:], op=ALU.pow
+            )
+
+        def normalise(r):
+            for i in range(r * RUN, (r + 1) * RUN):
+                xn[i] = front.tile([P, D], BF16, name="xn")
+                nc.vector.tensor_scalar(
+                    out=xn[i][:],
+                    in0=x_tile(i),
+                    scalar1=rnorm[:, i : i + 1],
+                    scalar2=g_f32[:],
+                    op0=ALU.mult,
+                    op1=ALU.mult,
+                )
+
+        def transpose_x(r):
+            x_banks[r] = []
+            for i in range(r * RUN, (r + 1) * RUN):
+                xn_words = xn[i][:].bitcast(F32)
+                bank = psum_t.tile([P, WORD_BLOCKS, P], F32, name="bank_t")
+                for c in range(PASSES):
+                    for w in range(2):
+                        nc.tensor.transpose(
+                            bank[:, 2 * c + w, :],
+                            xn_words[:, 2 * c * P + w : 2 * (c + 1) * P : 2],
+                            ident[:],
+                        )
+                x_banks[r].append(bank)
+
+        def copy_out_x(r):
+            grouped[r] = front.tile(
+                [P, PASSES * RUN_TOKENS * PACK], BF16, name="grouped", align_bytes=64
+            )
+            words = grouped[r][:].bitcast(F32).rearrange(
+                "p (c s t w) -> p c s t w", c=PASSES, s=RUN, w=2
+            )
+            for s, bank in enumerate(x_banks[r]):
+                nc.vector.tensor_copy(
+                    out=words[:, :, s, :, :],
+                    in_=bank[:].rearrange("p (c w) t -> p c t w", w=2),
+                )
+
+        def quantise_x(r):
+            x_codes[r] = front.tile(
+                [P, PASSES * RUN_TOKENS], U32, name="x_codes", align_bytes=64
+            )
+            x_scales[r] = front.tile(
+                [P, PASSES * RUN_TOKENS], U8, name="x_scales", align_bytes=64
+            )
+            nc.vector.quantize_mx(
+                out=x_codes[r][:].bitcast(FP8X4), scales=x_scales[r][:], in_=grouped[r][:]
+            )
+
+        def w_operand(c, first, width):
+            cols = slice(first, first + width)
+            return w_codes[:, c, cols], w_scales[:, c, cols]
+
+        def x_operand(r, c, first, width):
+            cols = slice(c * RUN_TOKENS + first, c * RUN_TOKENS + first + width)
+            return x_codes[r][:, cols], x_scales[r][:, cols]
+
+        def mx_pass(out, c, stationary, moving):
+            nc.tensor.matmul_mx(
+                out=out,
+                lhsT=stationary[0].bitcast(FP8X4),
+                lhsT_scale=stationary[1],
+                rhs=moving[0].bitcast(FP8X4),
+                rhs_scale=moving[1],
+                start=(c == 0),
+                stop=(c == PASSES - 1),
+            )
+
+        def project_base(r):
+            base_ps = psum_base.tile([P, BASE_BLOCKS, RUN_TOKENS], F32)
+            for b in range(BASE_BLOCKS):
+                for c in range(PASSES):
+                    mx_pass(
+                        base_ps[:, b, :],
+                        c,
+                        w_operand(c, 2 * H + b * P, P),
+                        x_operand(r, c, 0, RUN_TOKENS),
+                    )
+            base_t = back.tile([P, BASE_BLOCKS, RUN_TOKENS], F32)
+            qk_t[r] = back.tile([P, 2, BASE_BLOCKS, RUN_TOKENS], F32, name="qk_t", bufs=4)
+            for b in range(BASE_BLOCKS):
+                nc.scalar.activation(
+                    out=base_t[:, b, :],
+                    in_=base_ps[:, b, :],
+                    func=ACT.Silu,
+                    bias=base_const(BIAS_ROW, 0, b),
+                )
+                for a in range(2):
+                    nc.gpsimd.tensor_scalar(
+                        out=qk_t[r][:, a, b, :],
+                        in0=base_t[:, b, :],
+                        scalar1=base_const(GAMMA_ROW, a, b),
+                        scalar2=base_const(BETA_ROW, a, b),
+                        op0=ALU.mult,
+                        op1=ALU.add,
+                    )
+
+        def project_uv(r):
+            z[r] = back.tile([P, RUN, 2 * H], F32, name="z")
+            tail = psum_tail.tile([P, RUN, N_TAIL], F32)
+            for s in range(RUN):
+                head = psum_head.tile([P, N_BANK], F32)
+                for out, first, width in ((head[:], 0, N_BANK), (tail[:, s, :], N_BANK, N_TAIL)):
+                    for c in range(PASSES):
+                        mx_pass(out, c, x_operand(r, c, s * P, P), w_operand(c, first, width))
+                nc.vector.tensor_tensor(
+                    out=z[r][:, s, 0:N_BANK], in0=head[:], in1=uv_bias[:, 0:N_BANK], op=ALU.add
+                )
+            nc.vector.tensor_tensor(
+                out=z[r][:, :, N_BANK : 2 * H],
+                in0=tail[:],
+                in1=uv_bias[:, N_BANK : 2 * H].unsqueeze(1).to_broadcast([P, RUN, N_TAIL]),
+                op=ALU.add,
+            )
+
+        def finish_uv(r):
+            for dram, first in ((u_rows, 0), (v_rows, H)):
+                uv_out = outs.tile([P, RUN, H], F32, bufs=6)
+                nc.scalar.activation(
+                    out=uv_out[:], in_=z[r][:, :, first : first + H], func=ACT.Silu
+                )
+                nc.sync.dma_start(out=run_rows(dram, r), in_=uv_out[:])
+
+        def transpose_qk(r):
+            qk_banks[r] = []
+            for a in range(2):
+                bank = psum_t.tile([P, RUN, S], F32, name="bank_t")
+                for s in range(RUN):
+                    for b in range(BASE_BLOCKS):
+                        nc.tensor.transpose(
+                            bank[:, s, b * P : (b + 1) * P],
+                            qk_t[r][:, a, b, s * P : (s + 1) * P],
+                            ident[:],
+                        )
+                qk_banks[r].append(bank)
+
+        def copy_out_qk(r):
+            q_out = outs.tile([P, RUN, S], F32)
+            nc.vector.tensor_copy(out=q_out[:], in_=qk_banks[r][0][:])
+            nc.sync.dma_start(out=run_rows(q_rows, r), in_=q_out[:])
+            k_out = outs.tile([P, RUN, S], F32)
+            if r % 2 == 0:
+                nc.scalar.copy(out=k_out[:], in_=qk_banks[r][1][:])
+            else:
+                nc.vector.tensor_copy(out=k_out[:], in_=qk_banks[r][1][:])
+            nc.sync.dma_start(out=run_rows(k_rows, r), in_=k_out[:])
+
+        norm(0)
+        group_w(0)
+        normalise(0)
+        transpose_x(0)
+        quantise_w(0)
+        norm(1)
+        group_w(1)
+        copy_out_x(0)
+        normalise(1)
+        quantise_x(0)
+        quantise_w(1)
+        norm(2)
+
+        for r in range(RUNS + 2):
+            if 1 <= r <= RUNS:
+                finish_uv(r - 1)
+            if r + 1 < RUNS:
+                transpose_x(r + 1)
+            if r >= 2:
+                transpose_qk(r - 2)
+            if r + 1 < RUNS:
+                copy_out_x(r + 1)
+            if r >= 2:
+                copy_out_qk(r - 2)
+            if r + 1 < RUNS:
+                quantise_x(r + 1)
+            if r + 2 < RUNS:
+                normalise(r + 2)
+            if r < RUNS:
+                project_base(r)
+                project_uv(r)
+            if r + 3 < RUNS:
+                norm(r + 3)

@@ -211,8 +211,8 @@ def tile_gatedattentionunit_pa_t_kernel(
             for i in range(r * RUN, (r + 1) * RUN):
                 xn[i] = front.tile([P, D], BF16, name="xn")
                 nc.vector.tensor_scalar(
-                    out=xn[i][:],
-                    in0=x_tile(i),
+                    out=xn[i][:].rearrange("p (w m e) -> p w m e", w=2, e=2),
+                    in0=x_tile(i).rearrange("p (m w e) -> p w m e", w=2, e=2),
                     scalar1=rnorm[:, i : i + 1],
                     scalar2=g_f32[:],
                     op0=ALU.mult,
@@ -226,10 +226,9 @@ def tile_gatedattentionunit_pa_t_kernel(
                 bank = psum_t.tile([P, WORD_BLOCKS, P], F32, name="bank_t")
                 for c in range(PASSES):
                     for w in range(2):
+                        first = (w * PASSES + c) * P
                         nc.tensor.transpose(
-                            bank[:, 2 * c + w, :],
-                            xn_words[:, 2 * c * P + w : 2 * (c + 1) * P : 2],
-                            ident[:],
+                            bank[:, 2 * c + w, :], xn_words[:, first : first + P], ident[:]
                         )
                 x_banks[r].append(bank)
 

@@ -124,22 +124,24 @@ def tile_gatedattentionunit_pa_t_kernel(
         ones = const.tile([P, P], BF16)
         nc.vector.memset(ones[:], 1.0)
         uv_bias = const.tile([P, 2 * H], F32)
-        for first, width in ((0, N_BANK), (N_BANK, N_TAIL)):
-            spread = psum_head.tile([P, N_BANK], F32, name="head")
-            nc.tensor.matmul(
-                out=spread[:, 0:width],
-                lhsT=ones[:],
-                rhs=uv_bias_row[:, first : first + width],
-                start=True,
-                stop=True,
-            )
-            nc.vector.tensor_copy(
-                out=uv_bias[:, first : first + width], in_=spread[:, 0:width]
-            )
-        base_cols_ps = psum_t.tile([P, P], BF16, name="bank_t")
-        nc.tensor.transpose(base_cols_ps[:], base_rows[:], ident_bf[:])
         base_cols = const.tile([P, CONST_ROWS], F32)
-        nc.vector.tensor_copy(out=base_cols[:], in_=base_cols_ps[:, 0:CONST_ROWS])
+
+        def spread_constants():
+            for first, width in ((0, N_BANK), (N_BANK, N_TAIL)):
+                spread = psum_head.tile([P, N_BANK], F32, name="head")
+                nc.tensor.matmul(
+                    out=spread[:, 0:width],
+                    lhsT=ones[:],
+                    rhs=uv_bias_row[:, first : first + width],
+                    start=True,
+                    stop=True,
+                )
+                nc.vector.tensor_copy(
+                    out=uv_bias[:, first : first + width], in_=spread[:, 0:width]
+                )
+            base_cols_ps = psum_base.tile([P, P], BF16, name="base_ps")
+            nc.tensor.transpose(base_cols_ps[:], base_rows[:], ident_bf[:])
+            nc.vector.tensor_copy(out=base_cols[:], in_=base_cols_ps[:, 0:CONST_ROWS])
 
         def base_const(first_row, a, b):
             row = first_row + a * BASE_BLOCKS + b
@@ -180,20 +182,23 @@ def tile_gatedattentionunit_pa_t_kernel(
         qk_t = {}
         qk_banks = {}
         grouped = {}
+        base_ps = {}
+        base_t = {}
+        heads = {}
+        tails = {}
         z = {}
 
         def x_tile(i):
             return x_sb[i // RUN][:, i % RUN, :]
 
-        def norm(r):
-            for i in range(r * RUN, (r + 1) * RUN):
-                squares = front.tile([P, D], BF16, bufs=2)
-                nc.scalar.activation(
-                    out=squares[:],
-                    in_=x_tile(i),
-                    func=ACT.Square,
-                    accum_out=sumsq[:, i : i + 1],
-                )
+        def square(r, s):
+            i = r * RUN + s
+            squares = front.tile([P, D], BF16, bufs=2)
+            nc.scalar.activation(
+                out=squares[:], in_=x_tile(i), func=ACT.Square, accum_out=sumsq[:, i : i + 1]
+            )
+
+        def finish_norm(r):
             cols = slice(r * RUN, (r + 1) * RUN)
             nc.gpsimd.tensor_scalar(
                 out=meansq[:, cols],
@@ -207,43 +212,40 @@ def tile_gatedattentionunit_pa_t_kernel(
                 out=rnorm[:, cols], in0=meansq[:, cols], in1=neg_half[:], op=ALU.pow
             )
 
-        def normalise(r):
-            for i in range(r * RUN, (r + 1) * RUN):
-                xn[i] = front.tile([P, D], BF16, name="xn")
-                nc.vector.tensor_scalar(
-                    out=xn[i][:].rearrange("p (w m e) -> p w m e", w=2, e=2),
-                    in0=x_tile(i).rearrange("p (m w e) -> p w m e", w=2, e=2),
-                    scalar1=rnorm[:, i : i + 1],
-                    scalar2=g_f32[:],
-                    op0=ALU.mult,
-                    op1=ALU.mult,
-                )
-
-        def transpose_x(r):
-            x_banks[r] = []
-            for i in range(r * RUN, (r + 1) * RUN):
-                xn_words = xn[i][:].bitcast(F32)
-                bank = psum_t.tile([P, WORD_BLOCKS, P], F32, name="bank_t")
-                for c in range(PASSES):
-                    for w in range(2):
-                        first = (w * PASSES + c) * P
-                        nc.tensor.transpose(
-                            bank[:, 2 * c + w, :], xn_words[:, first : first + P], ident[:]
-                        )
-                x_banks[r].append(bank)
-
-        def copy_out_x(r):
-            grouped[r] = front.tile(
-                [P, PASSES * RUN_TOKENS * PACK], BF16, name="grouped", align_bytes=64
+        def normalise(r, s):
+            i = r * RUN + s
+            xn[i] = front.tile([P, D], BF16, name="xn")
+            nc.vector.tensor_scalar(
+                out=xn[i][:].rearrange("p (w m e) -> p w m e", w=2, e=2),
+                in0=x_tile(i).rearrange("p (m w e) -> p w m e", w=2, e=2),
+                scalar1=rnorm[:, i : i + 1],
+                scalar2=g_f32[:],
+                op0=ALU.mult,
+                op1=ALU.mult,
             )
+
+        def transpose_x(r, s):
+            xn_words = xn[r * RUN + s][:].bitcast(F32)
+            x_banks[r, s] = psum_t.tile([P, WORD_BLOCKS, P], F32, name="bank_t")
+            for c in range(PASSES):
+                for w in range(2):
+                    first = (w * PASSES + c) * P
+                    nc.tensor.transpose(
+                        x_banks[r, s][:, 2 * c + w, :], xn_words[:, first : first + P], ident[:]
+                    )
+
+        def copy_out_x(r, s):
+            if s == 0:
+                grouped[r] = front.tile(
+                    [P, PASSES * RUN_TOKENS * PACK], BF16, name="grouped", align_bytes=64
+                )
             words = grouped[r][:].bitcast(F32).rearrange(
                 "p (c s t w) -> p c s t w", c=PASSES, s=RUN, w=2
             )
-            for s, bank in enumerate(x_banks[r]):
-                nc.vector.tensor_copy(
-                    out=words[:, :, s, :, :],
-                    in_=bank[:].rearrange("p (c w) t -> p c t w", w=2),
-                )
+            nc.vector.tensor_copy(
+                out=words[:, :, s, :, :],
+                in_=x_banks[r, s][:].rearrange("p (c w) t -> p c t w", w=2),
+            )
 
         def quantise_x(r):
             x_codes[r] = front.tile(
@@ -276,114 +278,151 @@ def tile_gatedattentionunit_pa_t_kernel(
             )
 
         def project_base(r):
-            base_ps = psum_base.tile([P, BASE_BLOCKS, RUN_TOKENS], F32)
+            base_ps[r] = psum_base.tile([P, BASE_BLOCKS, RUN_TOKENS], F32, name="base_ps")
             for b in range(BASE_BLOCKS):
                 for c in range(PASSES):
                     mx_pass(
-                        base_ps[:, b, :],
+                        base_ps[r][:, b, :],
                         c,
                         w_operand(c, 2 * H + b * P, P),
                         x_operand(r, c, 0, RUN_TOKENS),
                     )
-            base_t = back.tile([P, BASE_BLOCKS, RUN_TOKENS], F32)
-            qk_t[r] = back.tile([P, 2, BASE_BLOCKS, RUN_TOKENS], F32, name="qk_t", bufs=4)
+
+        def silu_base(r):
+            base_t[r] = back.tile([P, BASE_BLOCKS, RUN_TOKENS], F32, name="base_t")
             for b in range(BASE_BLOCKS):
                 nc.scalar.activation(
-                    out=base_t[:, b, :],
-                    in_=base_ps[:, b, :],
+                    out=base_t[r][:, b, :],
+                    in_=base_ps[r][:, b, :],
                     func=ACT.Silu,
                     bias=base_const(BIAS_ROW, 0, b),
                 )
-                for a in range(2):
+
+        def affine_qk(r):
+            qk_t[r] = back.tile([P, 2, BASE_BLOCKS, RUN_TOKENS], F32, name="qk_t")
+            for a in range(2):
+                for b in range(BASE_BLOCKS):
                     nc.gpsimd.tensor_scalar(
                         out=qk_t[r][:, a, b, :],
-                        in0=base_t[:, b, :],
+                        in0=base_t[r][:, b, :],
                         scalar1=base_const(GAMMA_ROW, a, b),
                         scalar2=base_const(BETA_ROW, a, b),
                         op0=ALU.mult,
                         op1=ALU.add,
                     )
 
-        def project_uv(r):
-            z[r] = back.tile([P, RUN, 2 * H], F32, name="z")
-            tail = psum_tail.tile([P, RUN, N_TAIL], F32)
-            for s in range(RUN):
-                head = psum_head.tile([P, N_BANK], F32)
-                for out, first, width in ((head[:], 0, N_BANK), (tail[:, s, :], N_BANK, N_TAIL)):
-                    for c in range(PASSES):
-                        mx_pass(out, c, x_operand(r, c, s * P, P), w_operand(c, first, width))
-                nc.vector.tensor_tensor(
-                    out=z[r][:, s, 0:N_BANK], in0=head[:], in1=uv_bias[:, 0:N_BANK], op=ALU.add
-                )
+        def project_uv(r, s):
+            if s == 0:
+                tails[r] = psum_tail.tile([P, RUN, N_TAIL], F32, name="tail")
+            heads[r, s] = psum_head.tile([P, N_BANK], F32, name="head")
+            for out, first, width in (
+                (heads[r, s][:], 0, N_BANK),
+                (tails[r][:, s, :], N_BANK, N_TAIL),
+            ):
+                for c in range(PASSES):
+                    mx_pass(out, c, x_operand(r, c, s * P, P), w_operand(c, first, width))
+
+        def add_head(r, s):
+            if s == 0:
+                z[r] = back.tile([P, RUN, 2 * H], F32, name="z")
+            nc.vector.tensor_tensor(
+                out=z[r][:, s, 0:N_BANK], in0=heads[r, s][:], in1=uv_bias[:, 0:N_BANK], op=ALU.add
+            )
+
+        def add_tail(r):
             nc.vector.tensor_tensor(
                 out=z[r][:, :, N_BANK : 2 * H],
-                in0=tail[:],
+                in0=tails[r][:],
                 in1=uv_bias[:, N_BANK : 2 * H].unsqueeze(1).to_broadcast([P, RUN, N_TAIL]),
                 op=ALU.add,
             )
 
-        def finish_uv(r):
-            for dram, first in ((u_rows, 0), (v_rows, H)):
-                uv_out = outs.tile([P, RUN, H], F32, bufs=6)
-                nc.scalar.activation(
-                    out=uv_out[:], in_=z[r][:, :, first : first + H], func=ACT.Silu
-                )
-                nc.sync.dma_start(out=run_rows(dram, r), in_=uv_out[:])
+        def finish_uv(r, a):
+            uv_out = outs.tile([P, RUN, H], F32, bufs=6)
+            nc.scalar.activation(
+                out=uv_out[:], in_=z[r][:, :, a * H : (a + 1) * H], func=ACT.Silu
+            )
+            nc.sync.dma_start(out=run_rows((u_rows, v_rows)[a], r), in_=uv_out[:])
 
-        def transpose_qk(r):
-            qk_banks[r] = []
-            for a in range(2):
-                bank = psum_t.tile([P, RUN, S], F32, name="bank_t")
-                for s in range(RUN):
-                    for b in range(BASE_BLOCKS):
-                        nc.tensor.transpose(
-                            bank[:, s, b * P : (b + 1) * P],
-                            qk_t[r][:, a, b, s * P : (s + 1) * P],
-                            ident[:],
-                        )
-                qk_banks[r].append(bank)
+        def transpose_qk(r, a):
+            qk_banks[r, a] = psum_t.tile([P, RUN, S], F32, name="bank_t")
+            for s in range(RUN):
+                for b in range(BASE_BLOCKS):
+                    nc.tensor.transpose(
+                        qk_banks[r, a][:, s, b * P : (b + 1) * P],
+                        qk_t[r][:, a, b, s * P : (s + 1) * P],
+                        ident[:],
+                    )
 
-        def copy_out_qk(r):
-            q_out = outs.tile([P, RUN, S], F32)
-            nc.vector.tensor_copy(out=q_out[:], in_=qk_banks[r][0][:])
-            nc.sync.dma_start(out=run_rows(q_rows, r), in_=q_out[:])
-            k_out = outs.tile([P, RUN, S], F32)
-            if r % 2 == 0:
-                nc.scalar.copy(out=k_out[:], in_=qk_banks[r][1][:])
+        def copy_out_qk(r, a):
+            qk_out = outs.tile([P, RUN, S], F32, name="qk_out", bufs=6)
+            if a == 1 and r % 2 == 0:
+                nc.scalar.copy(out=qk_out[:], in_=qk_banks[r, a][:])
             else:
-                nc.vector.tensor_copy(out=k_out[:], in_=qk_banks[r][1][:])
-            nc.sync.dma_start(out=run_rows(k_rows, r), in_=k_out[:])
+                nc.vector.tensor_copy(out=qk_out[:], in_=qk_banks[r, a][:])
+            nc.sync.dma_start(out=run_rows((q_rows, k_rows)[a], r), in_=qk_out[:])
+
+        def norm(r):
+            for s in range(RUN):
+                square(r, s)
+            finish_norm(r)
 
         norm(0)
         group_w(0)
-        normalise(0)
-        transpose_x(0)
+        for s in range(RUN):
+            normalise(0, s)
+        for s in range(RUN):
+            transpose_x(0, s)
         quantise_w(0)
         norm(1)
         group_w(1)
-        copy_out_x(0)
-        normalise(1)
+        for s in range(RUN):
+            copy_out_x(0, s)
+        for s in range(RUN):
+            normalise(1, s)
+        for s in range(RUN):
+            transpose_x(1, s)
         quantise_x(0)
         quantise_w(1)
+        spread_constants()
         norm(2)
 
-        for r in range(RUNS + 2):
+        for r in range(RUNS + 3):
             if 1 <= r <= RUNS:
-                finish_uv(r - 1)
+                affine_qk(r - 1)
+                add_head(r - 1, 1)
+            if r + 3 < RUNS:
+                for s in range(RUN):
+                    square(r + 3, s)
             if r + 1 < RUNS:
-                transpose_x(r + 1)
-            if r >= 2:
-                transpose_qk(r - 2)
-            if r + 1 < RUNS:
-                copy_out_x(r + 1)
-            if r >= 2:
-                copy_out_qk(r - 2)
+                for s in range(RUN):
+                    copy_out_x(r + 1, s)
+            if r >= 3:
+                copy_out_qk(r - 3, 0)
+            if r < RUNS:
+                project_uv(r, 0)
+                project_base(r)
+                project_uv(r, 1)
+                add_head(r, 0)
+            if 1 <= r <= RUNS:
+                for a in range(2):
+                    finish_uv(r - 1, a)
+            if r >= 3:
+                copy_out_qk(r - 3, 1)
+            if r + 2 < RUNS:
+                for s in range(RUN):
+                    normalise(r + 2, s)
             if r + 1 < RUNS:
                 quantise_x(r + 1)
-            if r + 2 < RUNS:
-                normalise(r + 2)
             if r < RUNS:
-                project_base(r)
-                project_uv(r)
+                add_tail(r)
+            if r + 2 < RUNS:
+                for s in range(RUN):
+                    transpose_x(r + 2, s)
+            if 2 <= r < RUNS + 2:
+                for a in range(2):
+                    transpose_qk(r - 2, a)
+            if r < RUNS:
+                silu_base(r)
             if r + 3 < RUNS:
-                norm(r + 3)
+                finish_norm(r + 3)

@@ -70,7 +70,11 @@ def tile_gatedattentionunit_pa_t_kernel(
 
         def load_x(r):
             x_run = x_pool.tile([P, RUN, D], BF16, name="x_run%d" % r)
-            nc.sync.dma_start(out=x_run[:], in_=run_rows(x_rows, r))
+            if r == 0:
+                for s in range(RUN):
+                    nc.sync.dma_start(out=x_run[:, s, :], in_=run_rows(x_rows, r)[:, s, :])
+            else:
+                nc.sync.dma_start(out=x_run[:], in_=run_rows(x_rows, r))
             return x_run
 
         w_raw = const.tile([P, PASSES, PACK, E], BF16)
@@ -81,15 +85,19 @@ def tile_gatedattentionunit_pa_t_kernel(
                 in_=W_uv[c * K_PASS : (c + 1) * K_PASS, :].rearrange("(p j) n -> p j n", j=PACK),
             )
 
-        x_sb = [load_x(0)]
+        x_sb = [load_x(0), load_x(1)]
         load_w(0)
-        x_sb.append(load_x(1))
         load_w(1)
         for r in range(2, RUNS):
             x_sb.append(load_x(r))
 
         g_bf = const.tile([P, 1], BF16)
         nc.scalar.dma_start(out=g_bf[:], in_=g.partition_broadcast(P))
+
+        warm = const.tile([P, 1], F32)
+        nc.vector.memset(warm[:], 0.0)
+        nc.scalar.activation(out=warm[:], in_=warm[:], func=ACT.Silu)
+
         uv_bias_row = const.tile([P, 2 * H], BF16)
         nc.vector.memset(uv_bias_row[:], 0.0)
         nc.scalar.dma_start(out=uv_bias_row[0:1, :], in_=b_uv[0 : 2 * H].unsqueeze(0))
@@ -108,16 +116,12 @@ def tile_gatedattentionunit_pa_t_kernel(
             in_=beta.rearrange("a (b n) -> (a b) n", n=P),
         )
 
-        warm = const.tile([P, 1], F32)
-        nc.vector.memset(warm[:], 0.0)
-        nc.scalar.activation(out=warm[:], in_=warm[:], func=ACT.Silu)
-
+        neg_half = const.tile([P, RUN], F32)
+        nc.gpsimd.memset(neg_half[:], -0.5)
         ident = const.tile([P, P], F32)
         make_identity(nc, ident[:])
         ident_bf = const.tile([P, P], BF16)
         make_identity(nc, ident_bf[:])
-        neg_half = const.tile([P, RUN], F32)
-        nc.gpsimd.memset(neg_half[:], -0.5)
         g_f32 = const.tile([P, 1], F32)
         nc.vector.tensor_copy(out=g_f32[:], in_=g_bf[:])
 
@@ -151,26 +155,24 @@ def tile_gatedattentionunit_pa_t_kernel(
         w_scales = const.tile([P, PASSES, E], U8, align_bytes=64)
         w_grouped = {}
 
-        def group_w(c):
-            for half, copy in enumerate((nc.vector.tensor_copy, nc.scalar.copy)):
-                w_grouped[c, half] = w_stage.tile(
-                    [P, N_BANK, PACK], BF16, name="w_grouped", align_bytes=64
-                )
-                copy(
-                    out=w_grouped[c, half][:].rearrange("p (n m) j -> p n j m", m=4),
-                    in_=w_raw[:, c, :, half * N_BANK : (half + 1) * N_BANK].rearrange(
-                        "p j (n m) -> p n j m", m=4
-                    ),
-                )
+        def group_w(c, half, copy):
+            w_grouped[c, half] = w_stage.tile(
+                [P, N_BANK, PACK], BF16, name="w_grouped", align_bytes=64
+            )
+            copy(
+                out=w_grouped[c, half][:].rearrange("p (n m) j -> p n j m", m=4),
+                in_=w_raw[:, c, :, half * N_BANK : (half + 1) * N_BANK].rearrange(
+                    "p j (n m) -> p n j m", m=4
+                ),
+            )
 
-        def quantise_w(c):
-            for half in range(E // N_BANK):
-                cols = slice(half * N_BANK, (half + 1) * N_BANK)
-                nc.vector.quantize_mx(
-                    out=w_codes[:, c, cols].bitcast(FP8X4),
-                    scales=w_scales[:, c, cols],
-                    in_=w_grouped[c, half][:].rearrange("p n j -> p (n j)"),
-                )
+        def quantise_w(c, half):
+            cols = slice(half * N_BANK, (half + 1) * N_BANK)
+            nc.vector.quantize_mx(
+                out=w_codes[:, c, cols].bitcast(FP8X4),
+                scales=w_scales[:, c, cols],
+                in_=w_grouped[c, half][:].rearrange("p n j -> p (n j)"),
+            )
 
         sumsq = const.tile([P, TILES], F32)
         meansq = const.tile([P, TILES], F32)
@@ -196,6 +198,19 @@ def tile_gatedattentionunit_pa_t_kernel(
             squares = front.tile([P, D], BF16, bufs=2)
             nc.scalar.activation(
                 out=squares[:], in_=x_tile(i), func=ACT.Square, accum_out=sumsq[:, i : i + 1]
+            )
+
+        def square_on_vector(r, s):
+            i = r * RUN + s
+            squares = front.tile([P, D], BF16, name="squares_v", bufs=1)
+            nc.vector.scalar_tensor_tensor(
+                out=squares[:],
+                in0=x_tile(i),
+                scalar=1.0,
+                in1=x_tile(i),
+                op0=ALU.mult,
+                op1=ALU.mult,
+                accum_out=sumsq[:, i : i + 1],
             )
 
         def finish_norm(r):
@@ -298,18 +313,17 @@ def tile_gatedattentionunit_pa_t_kernel(
                     bias=base_const(BIAS_ROW, 0, b),
                 )
 
-        def affine_qk(r):
-            qk_t[r] = back.tile([P, 2, BASE_BLOCKS, RUN_TOKENS], F32, name="qk_t")
-            for a in range(2):
-                for b in range(BASE_BLOCKS):
-                    nc.gpsimd.tensor_scalar(
-                        out=qk_t[r][:, a, b, :],
-                        in0=base_t[r][:, b, :],
-                        scalar1=base_const(GAMMA_ROW, a, b),
-                        scalar2=base_const(BETA_ROW, a, b),
-                        op0=ALU.mult,
-                        op1=ALU.add,
-                    )
+        def affine_qk(r, a, engine):
+            qk_t[r, a] = back.tile([P, BASE_BLOCKS, RUN_TOKENS], F32, name="qk_t", bufs=6)
+            for b in range(BASE_BLOCKS):
+                engine.tensor_scalar(
+                    out=qk_t[r, a][:, b, :],
+                    in0=base_t[r][:, b, :],
+                    scalar1=base_const(GAMMA_ROW, a, b),
+                    scalar2=base_const(BETA_ROW, a, b),
+                    op0=ALU.mult,
+                    op1=ALU.add,
+                )
 
         def project_uv(r, s):
             if s == 0:
@@ -350,13 +364,13 @@ def tile_gatedattentionunit_pa_t_kernel(
                 for b in range(BASE_BLOCKS):
                     nc.tensor.transpose(
                         qk_banks[r, a][:, s, b * P : (b + 1) * P],
-                        qk_t[r][:, a, b, s * P : (s + 1) * P],
+                        qk_t[r, a][:, b, s * P : (s + 1) * P],
                         ident[:],
                     )
 
         def copy_out_qk(r, a):
             qk_out = outs.tile([P, RUN, S], F32, name="qk_out", bufs=6)
-            if a == 1 and r % 2 == 0:
+            if a == 1 and r % 3 != 1:
                 nc.scalar.copy(out=qk_out[:], in_=qk_banks[r, a][:])
             else:
                 nc.vector.tensor_copy(out=qk_out[:], in_=qk_banks[r, a][:])
@@ -367,29 +381,38 @@ def tile_gatedattentionunit_pa_t_kernel(
                 square(r, s)
             finish_norm(r)
 
-        norm(0)
-        group_w(0)
+        square_on_vector(0, 0)
+        square(0, 1)
+        finish_norm(0)
+        square(1, 0)
+        square(1, 1)
+        finish_norm(1)
         for s in range(RUN):
             normalise(0, s)
         for s in range(RUN):
             transpose_x(0, s)
-        quantise_w(0)
-        norm(1)
-        group_w(1)
+        for c in range(PASSES):
+            group_w(c, 1, nc.scalar.copy)
+        group_w(0, 0, nc.vector.tensor_copy)
         for s in range(RUN):
             copy_out_x(0, s)
         for s in range(RUN):
             normalise(1, s)
         for s in range(RUN):
             transpose_x(1, s)
+        group_w(1, 0, nc.vector.tensor_copy)
+        quantise_w(0, 0)
+        quantise_w(0, 1)
         quantise_x(0)
-        quantise_w(1)
+        quantise_w(1, 0)
+        quantise_w(1, 1)
         spread_constants()
         norm(2)
 
-        for r in range(RUNS + 3):
+        for r in range(RUNS + 2):
             if 1 <= r <= RUNS:
-                affine_qk(r - 1)
+                for a in range(2):
+                    affine_qk(r - 1, a, nc.gpsimd)
                 add_head(r - 1, 1)
             if r + 3 < RUNS:
                 for s in range(RUN):
@@ -397,8 +420,8 @@ def tile_gatedattentionunit_pa_t_kernel(
             if r + 1 < RUNS:
                 for s in range(RUN):
                     copy_out_x(r + 1, s)
-            if r >= 3:
-                copy_out_qk(r - 3, 0)
+            if r >= 2:
+                copy_out_qk(r - 2, 0)
             if r < RUNS:
                 project_uv(r, 0)
                 project_base(r)
@@ -407,8 +430,8 @@ def tile_gatedattentionunit_pa_t_kernel(
             if 1 <= r <= RUNS:
                 for a in range(2):
                     finish_uv(r - 1, a)
-            if r >= 3:
-                copy_out_qk(r - 3, 1)
+            if r >= 2:
+                copy_out_qk(r - 2, 1)
             if r + 2 < RUNS:
                 for s in range(RUN):
                     normalise(r + 2, s)
@@ -419,9 +442,9 @@ def tile_gatedattentionunit_pa_t_kernel(
             if r + 2 < RUNS:
                 for s in range(RUN):
                     transpose_x(r + 2, s)
-            if 2 <= r < RUNS + 2:
+            if 1 <= r <= RUNS:
                 for a in range(2):
-                    transpose_qk(r - 2, a)
+                    transpose_qk(r - 1, a)
             if r < RUNS:
                 silu_base(r)
             if r + 3 < RUNS:

@@ -370,7 +370,7 @@ def tile_gatedattentionunit_pa_t_kernel(
 
         def copy_out_qk(r, a):
             qk_out = outs.tile([P, RUN, S], F32, name="qk_out", bufs=6)
-            if a == 1 and r % 3 != 1:
+            if (a == 1 and r % 3 != 1) or RUNS - 6 <= r < RUNS - 2:
                 nc.scalar.copy(out=qk_out[:], in_=qk_banks[r, a][:])
             else:
                 nc.vector.tensor_copy(out=qk_out[:], in_=qk_banks[r, a][:])
@@ -384,7 +384,7 @@ def tile_gatedattentionunit_pa_t_kernel(
         square_on_vector(0, 0)
         square(0, 1)
         finish_norm(0)
-        square(1, 0)
+        square_on_vector(1, 0)
         square(1, 1)
         finish_norm(1)
         for s in range(RUN):
@@ -408,15 +408,16 @@ def tile_gatedattentionunit_pa_t_kernel(
         quantise_w(1, 1)
         spread_constants()
         norm(2)
+        norm(3)
 
         for r in range(RUNS + 2):
             if 1 <= r <= RUNS:
                 for a in range(2):
                     affine_qk(r - 1, a, nc.gpsimd)
                 add_head(r - 1, 1)
-            if r + 3 < RUNS:
+            if r + 4 < RUNS:
                 for s in range(RUN):
-                    square(r + 3, s)
+                    square(r + 4, s)
             if r + 1 < RUNS:
                 for s in range(RUN):
                     copy_out_x(r + 1, s)
@@ -447,5 +448,5 @@ def tile_gatedattentionunit_pa_t_kernel(
                     transpose_qk(r - 1, a)
             if r < RUNS:
                 silu_base(r)
-            if r + 3 < RUNS:
-                finish_norm(r + 3)
+            if r + 4 < RUNS:
+                finish_norm(r + 4)

from contextlib import ExitStack

import concourse.mybir as mybir
from concourse.masks import make_identity

F32 = mybir.dt.float32
BF16 = mybir.dt.bfloat16
U32 = mybir.dt.uint32
U8 = mybir.dt.uint8
FP8X4 = mybir.dt.float8_e4m3fn_x4
ACT = mybir.ActivationFunctionType
ALU = mybir.AluOpType

P = 128
TOKENS = 4 * 1024
D = 1024
H = 384
S = 256
E = 2 * H + S
EPS = 1e-5

PACK = 4
K_PASS = PACK * P
PASSES = D // K_PASS
N_BANK = 512
N_TAIL = 2 * H - N_BANK
WORD_BLOCKS = D // 2 // P
BASE_BLOCKS = S // P

TILES = TOKENS // P
RUN = 2
RUN_TOKENS = RUN * P
RUNS = TILES // RUN

BIAS_ROW = 0
GAMMA_ROW = BIAS_ROW + BASE_BLOCKS
BETA_ROW = GAMMA_ROW + 2 * BASE_BLOCKS
CONST_ROWS = BETA_ROW + 2 * BASE_BLOCKS

FLOPS = 2 * TOKENS * D * E


def tile_gatedattentionunit_pa_t_kernel(
    tc, x, g, W_uv, b_uv, gamma, beta, out_0, out_1, out_2, out_3
):
    nc = tc.nc
    x_rows = x.flatten_outer_dims()
    u_rows = out_0.flatten_outer_dims()
    v_rows = out_1.flatten_outer_dims()
    q_rows = out_2.flatten_outer_dims()
    k_rows = out_3.flatten_outer_dims()

    with ExitStack() as stack:
        const = stack.enter_context(tc.tile_pool(name="const", bufs=1))
        x_pool = stack.enter_context(tc.tile_pool(name="x_pool", bufs=1))
        w_stage = stack.enter_context(tc.tile_pool(name="w_stage", bufs=4))
        front = stack.enter_context(tc.tile_pool(name="front", bufs=4))
        back = stack.enter_context(tc.tile_pool(name="back", bufs=3))
        outs = stack.enter_context(tc.tile_pool(name="outs", bufs=4))
        psum_t = stack.enter_context(tc.psum_pool(name="psum_t", bufs=4))
        psum_head = stack.enter_context(tc.psum_pool(name="psum_head", bufs=2))
        psum_tail = stack.enter_context(tc.psum_pool(name="psum_tail", bufs=1))
        psum_base = stack.enter_context(tc.psum_pool(name="psum_base", bufs=1))
        stack.enter_context(tc.manual_schedule())

        def run_rows(dram, r):
            return dram[r * RUN_TOKENS : (r + 1) * RUN_TOKENS, :].rearrange(
                "(p s) n -> p s n", s=RUN
            )

        def load_x(r):
            x_run = x_pool.tile([P, RUN, D], BF16, name="x_run%d" % r)
            if r == 0:
                for s in range(RUN):
                    nc.sync.dma_start(out=x_run[:, s, :], in_=run_rows(x_rows, r)[:, s, :])
            else:
                nc.sync.dma_start(out=x_run[:], in_=run_rows(x_rows, r))
            return x_run

        w_raw = const.tile([P, PASSES, PACK, E], BF16)

        def load_w(c):
            nc.sync.dma_start(
                out=w_raw[:, c, :, :],
                in_=W_uv[c * K_PASS : (c + 1) * K_PASS, :].rearrange("(p j) n -> p j n", j=PACK),
            )

        x_sb = [load_x(0), load_x(1)]
        load_w(0)
        load_w(1)
        for r in range(2, RUNS):
            x_sb.append(load_x(r))

        g_bf = const.tile([P, 1], BF16)
        nc.scalar.dma_start(out=g_bf[:], in_=g.partition_broadcast(P))

        warm = const.tile([P, 1], F32)
        nc.vector.memset(warm[:], 0.0)
        nc.scalar.activation(out=warm[:], in_=warm[:], func=ACT.Silu)

        uv_bias_row = const.tile([P, 2 * H], BF16)
        nc.vector.memset(uv_bias_row[:], 0.0)
        nc.scalar.dma_start(out=uv_bias_row[0:1, :], in_=b_uv[0 : 2 * H].unsqueeze(0))
        base_rows = const.tile([P, P], BF16)
        nc.vector.memset(base_rows[:], 0.0)
        nc.scalar.dma_start(
            out=base_rows[BIAS_ROW:GAMMA_ROW, :],
            in_=b_uv[2 * H : E].rearrange("(b n) -> b n", n=P),
        )
        nc.scalar.dma_start(
            out=base_rows[GAMMA_ROW:BETA_ROW, :],
            in_=gamma.rearrange("a (b n) -> (a b) n", n=P),
        )
        nc.scalar.dma_start(
            out=base_rows[BETA_ROW:CONST_ROWS, :],
            in_=beta.rearrange("a (b n) -> (a b) n", n=P),
        )

        neg_half = const.tile([P, RUN], F32)
        nc.gpsimd.memset(neg_half[:], -0.5)
        ident = const.tile([P, P], F32)
        make_identity(nc, ident[:])
        ident_bf = const.tile([P, P], BF16)
        make_identity(nc, ident_bf[:])
        g_f32 = const.tile([P, 1], F32)
        nc.vector.tensor_copy(out=g_f32[:], in_=g_bf[:])

        ones = const.tile([P, P], BF16)
        nc.vector.memset(ones[:], 1.0)
        uv_bias = const.tile([P, 2 * H], F32)
        base_cols = const.tile([P, CONST_ROWS], F32)

        def spread_constants():
            for first, width in ((0, N_BANK), (N_BANK, N_TAIL)):
                spread = psum_head.tile([P, N_BANK], F32, name="head")
                nc.tensor.matmul(
                    out=spread[:, 0:width],
                    lhsT=ones[:],
                    rhs=uv_bias_row[:, first : first + width],
                    start=True,
                    stop=True,
                )
                nc.vector.tensor_copy(
                    out=uv_bias[:, first : first + width], in_=spread[:, 0:width]
                )
            base_cols_ps = psum_base.tile([P, P], BF16, name="base_ps")
            nc.tensor.transpose(base_cols_ps[:], base_rows[:], ident_bf[:])
            nc.vector.tensor_copy(out=base_cols[:], in_=base_cols_ps[:, 0:CONST_ROWS])

        def base_const(first_row, a, b):
            row = first_row + a * BASE_BLOCKS + b
            return base_cols[:, row : row + 1]

        w_codes = const.tile([P, PASSES, E], U32, align_bytes=64)
        w_scales = const.tile([P, PASSES, E], U8, align_bytes=64)
        w_grouped = {}

        def group_w(c, half, copy):
            w_grouped[c, half] = w_stage.tile(
                [P, N_BANK, PACK], BF16, name="w_grouped", align_bytes=64
            )
            copy(
                out=w_grouped[c, half][:].rearrange("p (n m) j -> p n j m", m=4),
                in_=w_raw[:, c, :, half * N_BANK : (half + 1) * N_BANK].rearrange(
                    "p j (n m) -> p n j m", m=4
                ),
            )

        def quantise_w(c, half):
            cols = slice(half * N_BANK, (half + 1) * N_BANK)
            nc.vector.quantize_mx(
                out=w_codes[:, c, cols].bitcast(FP8X4),
                scales=w_scales[:, c, cols],
                in_=w_grouped[c, half][:].rearrange("p n j -> p (n j)"),
            )

        sumsq = const.tile([P, TILES], F32)
        meansq = const.tile([P, TILES], F32)
        rnorm = const.tile([P, TILES], F32)
        xn = {}
        x_banks = {}
        x_codes = {}
        x_scales = {}
        qk_t = {}
        qk_banks = {}
        grouped = {}
        base_ps = {}
        base_t = {}
        heads = {}
        tails = {}
        z = {}

        def x_tile(i):
            return x_sb[i // RUN][:, i % RUN, :]

        def square(r, s):
            i = r * RUN + s
            squares = front.tile([P, D], BF16, bufs=2)
            nc.scalar.activation(
                out=squares[:], in_=x_tile(i), func=ACT.Square, accum_out=sumsq[:, i : i + 1]
            )

        def square_on_vector(r, s):
            i = r * RUN + s
            squares = front.tile([P, D], BF16, name="squares_v", bufs=1)
            nc.vector.scalar_tensor_tensor(
                out=squares[:],
                in0=x_tile(i),
                scalar=1.0,
                in1=x_tile(i),
                op0=ALU.mult,
                op1=ALU.mult,
                accum_out=sumsq[:, i : i + 1],
            )

        def finish_norm(r):
            cols = slice(r * RUN, (r + 1) * RUN)
            nc.gpsimd.tensor_scalar(
                out=meansq[:, cols],
                in0=sumsq[:, cols],
                scalar1=1.0 / D,
                scalar2=EPS * EPS,
                op0=ALU.mult,
                op1=ALU.max,
            )
            nc.gpsimd.tensor_tensor(
                out=rnorm[:, cols], in0=meansq[:, cols], in1=neg_half[:], op=ALU.pow
            )

        def normalise(r, s):
            i = r * RUN + s
            xn[i] = front.tile([P, D], BF16, name="xn")
            nc.vector.tensor_scalar(
                out=xn[i][:].rearrange("p (w m e) -> p w m e", w=2, e=2),
                in0=x_tile(i).rearrange("p (m w e) -> p w m e", w=2, e=2),
                scalar1=rnorm[:, i : i + 1],
                scalar2=g_f32[:],
                op0=ALU.mult,
                op1=ALU.mult,
            )

        def transpose_x(r, s):
            xn_words = xn[r * RUN + s][:].bitcast(F32)
            x_banks[r, s] = psum_t.tile([P, WORD_BLOCKS, P], F32, name="bank_t")
            for c in range(PASSES):
                for w in range(2):
                    first = (w * PASSES + c) * P
                    nc.tensor.transpose(
                        x_banks[r, s][:, 2 * c + w, :], xn_words[:, first : first + P], ident[:]
                    )

        def copy_out_x(r, s):
            if s == 0:
                grouped[r] = front.tile(
                    [P, PASSES * RUN_TOKENS * PACK], BF16, name="grouped", align_bytes=64
                )
            words = grouped[r][:].bitcast(F32).rearrange(
                "p (c s t w) -> p c s t w", c=PASSES, s=RUN, w=2
            )
            nc.vector.tensor_copy(
                out=words[:, :, s, :, :],
                in_=x_banks[r, s][:].rearrange("p (c w) t -> p c t w", w=2),
            )

        def quantise_x(r):
            x_codes[r] = front.tile(
                [P, PASSES * RUN_TOKENS], U32, name="x_codes", align_bytes=64
            )
            x_scales[r] = front.tile(
                [P, PASSES * RUN_TOKENS], U8, name="x_scales", align_bytes=64
            )
            nc.vector.quantize_mx(
                out=x_codes[r][:].bitcast(FP8X4), scales=x_scales[r][:], in_=grouped[r][:]
            )

        def w_operand(c, first, width):
            cols = slice(first, first + width)
            return w_codes[:, c, cols], w_scales[:, c, cols]

        def x_operand(r, c, first, width):
            cols = slice(c * RUN_TOKENS + first, c * RUN_TOKENS + first + width)
            return x_codes[r][:, cols], x_scales[r][:, cols]

        def mx_pass(out, c, stationary, moving):
            nc.tensor.matmul_mx(
                out=out,
                lhsT=stationary[0].bitcast(FP8X4),
                lhsT_scale=stationary[1],
                rhs=moving[0].bitcast(FP8X4),
                rhs_scale=moving[1],
                start=(c == 0),
                stop=(c == PASSES - 1),
            )

        def project_base(r):
            base_ps[r] = psum_base.tile([P, BASE_BLOCKS, RUN_TOKENS], F32, name="base_ps")
            for b in range(BASE_BLOCKS):
                for c in range(PASSES):
                    mx_pass(
                        base_ps[r][:, b, :],
                        c,
                        w_operand(c, 2 * H + b * P, P),
                        x_operand(r, c, 0, RUN_TOKENS),
                    )

        def silu_base(r):
            base_t[r] = back.tile([P, BASE_BLOCKS, RUN_TOKENS], F32, name="base_t")
            for b in range(BASE_BLOCKS):
                nc.scalar.activation(
                    out=base_t[r][:, b, :],
                    in_=base_ps[r][:, b, :],
                    func=ACT.Silu,
                    bias=base_const(BIAS_ROW, 0, b),
                )

        def affine_qk(r, a, engine):
            qk_t[r, a] = back.tile([P, BASE_BLOCKS, RUN_TOKENS], F32, name="qk_t", bufs=6)
            for b in range(BASE_BLOCKS):
                engine.tensor_scalar(
                    out=qk_t[r, a][:, b, :],
                    in0=base_t[r][:, b, :],
                    scalar1=base_const(GAMMA_ROW, a, b),
                    scalar2=base_const(BETA_ROW, a, b),
                    op0=ALU.mult,
                    op1=ALU.add,
                )

        def project_uv(r, s):
            if s == 0:
                tails[r] = psum_tail.tile([P, RUN, N_TAIL], F32, name="tail")
            heads[r, s] = psum_head.tile([P, N_BANK], F32, name="head")
            for out, first, width in (
                (heads[r, s][:], 0, N_BANK),
                (tails[r][:, s, :], N_BANK, N_TAIL),
            ):
                for c in range(PASSES):
                    mx_pass(out, c, x_operand(r, c, s * P, P), w_operand(c, first, width))

        def add_head(r, s):
            if s == 0:
                z[r] = back.tile([P, RUN, 2 * H], F32, name="z")
            nc.vector.tensor_tensor(
                out=z[r][:, s, 0:N_BANK], in0=heads[r, s][:], in1=uv_bias[:, 0:N_BANK], op=ALU.add
            )

        def add_tail(r):
            nc.vector.tensor_tensor(
                out=z[r][:, :, N_BANK : 2 * H],
                in0=tails[r][:],
                in1=uv_bias[:, N_BANK : 2 * H].unsqueeze(1).to_broadcast([P, RUN, N_TAIL]),
                op=ALU.add,
            )

        def finish_uv(r, a):
            uv_out = outs.tile([P, RUN, H], F32, bufs=6)
            nc.scalar.activation(
                out=uv_out[:], in_=z[r][:, :, a * H : (a + 1) * H], func=ACT.Silu
            )
            nc.sync.dma_start(out=run_rows((u_rows, v_rows)[a], r), in_=uv_out[:])

        def transpose_qk(r, a):
            qk_banks[r, a] = psum_t.tile([P, RUN, S], F32, name="bank_t")
            for s in range(RUN):
                for b in range(BASE_BLOCKS):
                    nc.tensor.transpose(
                        qk_banks[r, a][:, s, b * P : (b + 1) * P],
                        qk_t[r, a][:, b, s * P : (s + 1) * P],
                        ident[:],
                    )

        def copy_out_qk(r, a):
            qk_out = outs.tile([P, RUN, S], F32, name="qk_out", bufs=6)
            if (a == 1 and r % 3 != 1) or RUNS - 6 <= r < RUNS - 2:
                nc.scalar.copy(out=qk_out[:], in_=qk_banks[r, a][:])
            else:
                nc.vector.tensor_copy(out=qk_out[:], in_=qk_banks[r, a][:])
            nc.sync.dma_start(out=run_rows((q_rows, k_rows)[a], r), in_=qk_out[:])

        def norm(r):
            for s in range(RUN):
                square(r, s)
            finish_norm(r)

        square_on_vector(0, 0)
        square(0, 1)
        finish_norm(0)
        square_on_vector(1, 0)
        square(1, 1)
        finish_norm(1)
        for s in range(RUN):
            normalise(0, s)
        for s in range(RUN):
            transpose_x(0, s)
        for c in range(PASSES):
            group_w(c, 1, nc.scalar.copy)
        group_w(0, 0, nc.vector.tensor_copy)
        for s in range(RUN):
            copy_out_x(0, s)
        for s in range(RUN):
            normalise(1, s)
        for s in range(RUN):
            transpose_x(1, s)
        group_w(1, 0, nc.vector.tensor_copy)
        quantise_w(0, 0)
        quantise_w(0, 1)
        quantise_x(0)
        quantise_w(1, 0)
        quantise_w(1, 1)
        spread_constants()
        norm(2)
        norm(3)

        for r in range(RUNS + 2):
            if 1 <= r <= RUNS:
                for a in range(2):
                    affine_qk(r - 1, a, nc.gpsimd)
                add_head(r - 1, 1)
            if r + 4 < RUNS:
                for s in range(RUN):
                    square(r + 4, s)
            if r + 1 < RUNS:
                for s in range(RUN):
                    copy_out_x(r + 1, s)
            if r >= 2:
                copy_out_qk(r - 2, 0)
            if r < RUNS:
                project_uv(r, 0)
                project_base(r)
                project_uv(r, 1)
                add_head(r, 0)
            if 1 <= r <= RUNS:
                for a in range(2):
                    finish_uv(r - 1, a)
            if r >= 2:
                copy_out_qk(r - 2, 1)
            if r + 2 < RUNS:
                for s in range(RUN):
                    normalise(r + 2, s)
            if r + 1 < RUNS:
                quantise_x(r + 1)
            if r < RUNS:
                add_tail(r)
            if r + 2 < RUNS:
                for s in range(RUN):
                    transpose_x(r + 2, s)
            if 1 <= r <= RUNS:
                for a in range(2):
                    transpose_qk(r - 1, a)
            if r < RUNS:
                silu_base(r)
            if r + 4 < RUNS:
                finish_norm(r + 4)
